import numpy as np
import ml_dtypes


def mxq(x, axis, fmt="e4m3"):
    dtype, down = {"e4m3": (ml_dtypes.float8_e4m3fn, 7), "e5m2": (ml_dtypes.float8_e5m2, 14)}[fmt]
    v = np.moveaxis(np.asarray(x, np.float32).astype(ml_dtypes.bfloat16).astype(np.float64), axis, -1)
    blocks = v.reshape(v.shape[:-1] + (-1, 32))
    amax = np.abs(blocks).max(-1, keepdims=True)
    byte = np.maximum(np.where(amax > 0, np.frexp(amax)[1] - 1 + 127, 0) - down, 1)
    scale = np.exp2(byte - 127.0)
    codes = (blocks / scale).astype(np.float32).astype(dtype).astype(np.float64)
    return np.moveaxis((codes * scale).reshape(v.shape), -1, axis)


WIDE = False


def mx_kscale(k):
    if not WIDE:
        return np.ones(k)
    levels = np.array([10, -10, 5, -5, 0])
    a = np.random.permutation(np.resize(levels, k // 512 * 4)).reshape(k // 512, 4)
    idx = np.arange(k)
    return np.exp2(a[idx // 512, idx % 128 // 32])


BF16 = ml_dtypes.bfloat16


def bf(x):
    return np.asarray(x, np.float32).astype(BF16)


def f64(x):
    return np.asarray(x).astype(np.float64)


B, F, H, C = 4096, 1024, 128, 10
EPS = 4.0 / 30.0
P_KEEP = 0.95


def setup_inputs():
    s = mx_kscale(F)
    ns = EPS / (6.0 * np.sqrt(H))
    return {"x1": bf(np.random.standard_normal((B, F)) * s),
            "x2": bf(np.random.standard_normal((B, F)) * s),
            "W1": bf(np.random.standard_normal((F, H)) / np.sqrt(F) / s[:, None]),
            "b1": bf(np.random.standard_normal(H) * 0.3),
            "W2": bf(np.random.standard_normal((F, H)) / np.sqrt(F) / s[:, None]),
            "b2": bf(np.random.standard_normal(H) * 0.3),
            "noise_std": bf(np.random.laplace(size=(B, H)) * ns),
            "rr_uniform": bf(np.random.uniform(size=H))}


def reference(x1, x2, W1, b1, W2, b2, noise_std, rr_uniform):
    out1 = (mxq(f64(x1), 1, "e4m3") @ mxq(f64(W1), 0, "e4m3")) + f64(b1)
    one_norm = np.sum(np.abs(out1), axis=1)
    sensitivity = np.max(one_norm) - np.min(one_norm)
    noise_mul = sensitivity / EPS
    out1 = out1 + f64(noise_std) * noise_mul
    rr_mask = np.where(f64(rr_uniform) < P_KEEP, 1.0, 0.0)
    out1 = out1 * rr_mask
    out2 = (mxq(f64(x2), 1, "e4m3") @ mxq(f64(W2), 0, "e4m3")) + f64(b2)
    return np.minimum(out1, out2)

@@ -1,0 +1,237 @@
+from contextlib import ExitStack
+
+import concourse.bass as bass
+import concourse.mybir as mybir
+import concourse.tile as tile
+from concourse.masks import make_identity
+
+F32 = mybir.dt.float32
+BF16 = mybir.dt.bfloat16
+U32 = mybir.dt.uint32
+U8 = mybir.dt.uint8
+FP8X4 = mybir.dt.float8_e4m3fn_x4
+ALU = mybir.AluOpType
+AX = mybir.AxisListType
+ACT = mybir.ActivationFunctionType
+
+P = 128
+B, F, H = 4096, 1024, 128
+T_ALL = B // P
+T_CH = 4
+N_CH = T_ALL // T_CH
+INV_EPS = 7.5
+P_KEEP = 0.95
+
+FLOPS = 2 * 2 * B * F * H
+
+
+def tile_splitnn_pa_t_kernel(tc, x1, x2, W1, b1, W2, b2, noise_std, rr_uniform, out):
+    nc = tc.nc
+    with ExitStack() as ctx:
+        const = ctx.enter_context(tc.tile_pool(name="const", bufs=1))
+        xpool = ctx.enter_context(tc.tile_pool(name="xpool", bufs=2 * N_CH))
+        gpool = ctx.enter_context(tc.tile_pool(name="gpool", bufs=3))
+        qpool = ctx.enter_context(tc.tile_pool(name="qpool", bufs=3))
+        opool = ctx.enter_context(tc.tile_pool(name="opool", bufs=3))
+        tpsum = ctx.enter_context(tc.psum_pool(name="tpsum", bufs=6))
+        apsum = ctx.enter_context(tc.psum_pool(name="apsum", bufs=2))
+        ctx.enter_context(tc.manual_schedule())
+
+        brow = const.tile([P, 512], BF16)
+        ones = const.tile([P, P], BF16)
+        nc.vector.memset(brow[:], 0.0)
+        nc.vector.memset(ones[:], 1.0)
+        nc.sync.dma_start(out=brow[0:1, 0:128], in_=b1.rearrange("(o h) -> o h", o=1))
+        nc.sync.dma_start(out=brow[0:1, 128:256], in_=b2.rearrange("(o h) -> o h", o=1))
+        nc.sync.dma_start(out=brow[0:1, 256:384], in_=rr_uniform.rearrange("(o h) -> o h", o=1))
+        wraws = []
+
+        def load_w(wi, W):
+            wraw = const.tile([P, 1024], BF16, name="wraw%d" % wi)
+            nc.sync.dma_start(
+                out=wraw[:].rearrange("p (s e h) -> p s e h", s=4, e=2),
+                in_=W.rearrange("(s q e) h -> q s e h", s=4, q=P, e=2),
+            )
+            wraws.append(wraw)
+
+        load_w(0, W1)
+
+        xs = []
+        nz = const.tile([P, T_ALL * H], BF16)
+        for xi, x in enumerate((x1, x2)):
+            xv = x.rearrange("(p t) k -> p t k", t=T_ALL)
+            for c in range(N_CH):
+                x_sb = xpool.tile([P, T_CH * F], BF16, tag="x", name="x%d_%d" % (xi, c))
+                nc.sync.dma_start(
+                    out=x_sb[:],
+                    in_=xv[:, c * T_CH : (c + 1) * T_CH, :].rearrange("p t k -> p (t k)"),
+                )
+                xs.append(x_sb)
+                if xi == 0 and c == 1:
+                    load_w(1, W2)
+            if xi == 0:
+                nc.sync.dma_start(out=nz[:], in_=noise_std.rearrange("(p t) h -> p (t h)", t=T_ALL))
+        out_v = out.rearrange("(p t) h -> p t h", t=T_ALL)
+
+        ident = const.tile([P, P], F32)
+        make_identity(nc, ident[:])
+
+        bc_ps = tpsum.tile([P, 512], F32, tag="tp", name="bc_ps")
+        nc.tensor.matmul(out=bc_ps[:], lhsT=ones[:], rhs=brow[:], start=True, stop=True)
+        b12 = const.tile([P, 256], F32)
+        keep = const.tile([P, H], F32)
+        nc.vector.tensor_copy(out=b12[:], in_=bc_ps[:, 0:256])
+        nc.vector.tensor_single_scalar(out=keep[:], in_=bc_ps[:, 256:384], scalar=P_KEEP, op=ALU.is_lt)
+        b1_b = b12[:, 0:128].unsqueeze(1).to_broadcast([P, T_CH, H])
+        b2_b = b12[:, 128:256].unsqueeze(1).to_broadcast([P, T_CH, H])
+        keep_b = keep[:].unsqueeze(1).to_broadcast([P, T_CH, H])
+
+        wcs = []
+
+        def prepare_w(wi):
+            wg = const.tile([P, 1024], BF16, name="wg%d" % wi, align_bytes=64)
+            nc.vector.tensor_copy(
+                out=wg[:].rearrange("p (g h t) -> p g h t", g=2, h=H, t=4),
+                in_=wraws[wi][:].rearrange("p (g t h) -> p g h t", g=2, t=4, h=H),
+            )
+            wc = const.tile([P, 256], U32, name="wc%d" % wi, align_bytes=64)
+            ws = const.tile([P, 256], U8, name="ws%d" % wi, align_bytes=64)
+            wcs.append((wg, wc, ws))
+
+        def quantise_w(wi):
+            wg, wc, ws = wcs[wi]
+            nc.vector.quantize_mx(out=wc[:].bitcast(FP8X4), scales=ws[:], in_=wg[:])
+
+        prepare_w(0)
+
+        a_all = const.tile([P, T_ALL * H], F32)
+        nrm = const.tile([P, T_ALL], F32)
+        mm = const.tile([P, 2], F32)
+        rep = const.tile([P, 256], F32)
+        gm = const.tile([P, 2], F32)
+        mul = const.tile([P, 1], F32)
+
+        quantise_w(0)
+
+        banks = {}
+        grps = {}
+        codes = {}
+        absd = {}
+
+        def transposes(i):
+            xw = xs[i][:].bitcast(F32)
+            for t in range(T_CH):
+                bank = tpsum.tile([P, 512], F32, tag="tp", name="tp%d_%d" % (i, t))
+                for s in range(4):
+                    col = t * 512 + s * P
+                    nc.tensor.transpose(bank[:, s * P : (s + 1) * P], xw[:, col : col + P], ident[:])
+                banks[(i, t)] = bank
+
+        def evacuate(i):
+            grp = gpool.tile([P, T_CH * F], BF16, tag="grp", name="grp%d" % i, align_bytes=64)
+            gw = grp[:].bitcast(F32)
+            for t in range(T_CH):
+                nc.scalar.copy(
+                    out=gw[:, t * 512 : (t + 1) * 512].rearrange("p (g r u) -> p g r u", g=2, r=P, u=2),
+                    in_=banks[(i, t)][:].rearrange("p (g u r) -> p g r u", g=2, u=2, r=P),
+                )
+            grps[i] = grp
+
+        def quantise(i):
+            cd = qpool.tile([P, T_CH * 256], U32, tag="cd", name="cd%d" % i, align_bytes=64)
+            sc = qpool.tile([P, T_CH * 256], U8, tag="sc", name="sc%d" % i, align_bytes=64)
+            nc.vector.quantize_mx(out=cd[:].bitcast(FP8X4), scales=sc[:], in_=grps[i][:])
+            codes[i] = (cd, sc)
+
+        def multiply(i):
+            cd, sc = codes[i]
+            wg, wc, ws = wcs[i // N_CH]
+            acc = apsum.tile([P, 512], F32, tag="acc", name="acc%d" % i)
+            for t in range(T_CH):
+                for g in range(2):
+                    col = (2 * t + g) * P
+                    nc.tensor.matmul_mx(
+                        out=acc[:, t * H : (t + 1) * H],
+                        lhsT=cd[:, col : col + P].bitcast(FP8X4),
+                        lhsT_scale=sc[:, col : col + P],
+                        rhs=wc[:, g * H : (g + 1) * H].bitcast(FP8X4),
+                        rhs_scale=ws[:, g * H : (g + 1) * H],
+                        start=(g == 0),
+                        stop=(g == 1),
+                    )
+            return acc
+
+        def three(ap):
+            return ap.rearrange("p (t h) -> p t h", t=T_CH)
+
+        def finish_client1(c, acc):
+            a_c = a_all[:, c * 512 : (c + 1) * 512]
+            nc.vector.tensor_tensor(out=three(a_c), in0=three(acc[:]), in1=b1_b, op=ALU.add)
+            ab = opool.tile([P, 512], F32, tag="ab", name="ab%d" % c)
+            nc.scalar.activation(out=ab[:], in_=a_c, func=ACT.Abs)
+            absd[c] = ab
+
+        def norms(c):
+            nc.vector.tensor_reduce(
+                out=nrm[:, c * T_CH : (c + 1) * T_CH], in_=three(absd[c][:]), axis=AX.X, op=ALU.add
+            )
+
+        def finish_client2(c, acc):
+            a_c = a_all[:, c * 512 : (c + 1) * 512]
+            nc.vector.scalar_tensor_tensor(
+                out=a_c,
+                in0=nz[:, c * 512 : (c + 1) * 512],
+                scalar=mul[:, 0:1],
+                in1=a_c,
+                op0=ALU.mult,
+                op1=ALU.add,
+            )
+            nc.vector.tensor_tensor(out=three(a_c), in0=three(a_c), in1=keep_b, op=ALU.mult)
+            o = opool.tile([P, 512], F32, tag="o", name="o%d" % c)
+            nc.vector.tensor_tensor(out=three(o[:]), in0=three(acc[:]), in1=b2_b, op=ALU.add)
+            nc.vector.tensor_tensor(out=o[:], in0=o[:], in1=a_c, op=ALU.min)
+            nc.sync.dma_start(out=out_v[:, c * T_CH : (c + 1) * T_CH, :], in_=three(o[:]))
+
+        n_all = 2 * N_CH
+        for i in range(n_all + 2):
+            if i < n_all:
+                transposes(i)
+                evacuate(i)
+            if i == N_CH + 2:
+                sp = tpsum.tile([P, 512], F32, tag="tp", name="sp")
+                nc.tensor.transpose(sp[:, 0:P], rep[:, 0:P], ident[:])
+                nc.tensor.transpose(sp[:, P : 2 * P], rep[:, P : 2 * P], ident[:])
+            if i == 3:
+                prepare_w(1)
+            if 1 <= i <= n_all:
+                quantise(i - 1)
+            if i == 3:
+                quantise_w(1)
+            if i == N_CH + 2:
+                nc.vector.tensor_reduce(out=gm[:, 0:1], in_=sp[:, 0:P], axis=AX.X, op=ALU.max)
+                nc.vector.tensor_reduce(out=gm[:, 1:2], in_=sp[:, P : 2 * P], axis=AX.X, op=ALU.min)
+                nc.vector.tensor_scalar(
+                    out=mul[:],
+                    in0=gm[:, 0:1],
+                    scalar1=gm[:, 1:2],
+                    scalar2=INV_EPS,
+                    op0=ALU.subtract,
+                    op1=ALU.mult,
+                )
+            if i >= 2:
+                j = i - 2
+                acc = multiply(j)
+                if j < N_CH:
+                    if j >= 1:
+                        norms(j - 1)
+                    finish_client1(j, acc)
+                else:
+                    finish_client2(j - N_CH, acc)
+                if j == N_CH - 1:
+                    norms(j)
+                    nc.vector.tensor_reduce(out=mm[:, 0:1], in_=nrm[:], axis=AX.X, op=ALU.max)
+                    nc.vector.tensor_reduce(out=mm[:, 1:2], in_=nrm[:], axis=AX.X, op=ALU.min)
+                    nc.vector.tensor_copy(
+                        out=rep[:].rearrange("p (s j) -> p s j", s=2),
+                        in_=mm[:].unsqueeze(2).to_broadcast([P, 2, P]),
+                    )

@@ -1,8 +1,6 @@
 from contextlib import ExitStack
 
-import concourse.bass as bass
 import concourse.mybir as mybir
-import concourse.tile as tile
 from concourse.masks import make_identity
 
 F32 = mybir.dt.float32
@@ -38,12 +36,9 @@ def tile_splitnn_pa_t_kernel(tc, x1, x2, W1, b1, W2, b2, noise_std, rr_uniform, 
         ctx.enter_context(tc.manual_schedule())
 
         brow = const.tile([P, 512], BF16)
-        ones = const.tile([P, P], BF16)
+        ones = const.tile([P, 256], BF16)
         nc.vector.memset(brow[:], 0.0)
         nc.vector.memset(ones[:], 1.0)
-        nc.sync.dma_start(out=brow[0:1, 0:128], in_=b1.rearrange("(o h) -> o h", o=1))
-        nc.sync.dma_start(out=brow[0:1, 128:256], in_=b2.rearrange("(o h) -> o h", o=1))
-        nc.sync.dma_start(out=brow[0:1, 256:384], in_=rr_uniform.rearrange("(o h) -> o h", o=1))
         wraws = []
 
         def load_w(wi, W):
@@ -54,20 +49,26 @@ def tile_splitnn_pa_t_kernel(tc, x1, x2, W1, b1, W2, b2, noise_std, rr_uniform, 
             )
             wraws.append(wraw)
 
-        load_w(0, W1)
-
         xs = []
         nz = const.tile([P, T_ALL * H], BF16)
         for xi, x in enumerate((x1, x2)):
             xv = x.rearrange("(p t) k -> p t k", t=T_ALL)
             for c in range(N_CH):
                 x_sb = xpool.tile([P, T_CH * F], BF16, tag="x", name="x%d_%d" % (xi, c))
-                nc.sync.dma_start(
-                    out=x_sb[:],
-                    in_=xv[:, c * T_CH : (c + 1) * T_CH, :].rearrange("p t k -> p (t k)"),
-                )
+                pieces = 4 if (xi == 0 and c < 2) else 1
+                tp_ = T_CH // pieces
+                for q in range(pieces):
+                    nc.sync.dma_start(
+                        out=x_sb[:, q * tp_ * F : (q + 1) * tp_ * F],
+                        in_=xv[:, c * T_CH + q * tp_ : c * T_CH + (q + 1) * tp_, :].rearrange("p t k -> p (t k)"),
+                    )
                 xs.append(x_sb)
-                if xi == 0 and c == 1:
+                if xi == 0 and c == 0:
+                    nc.sync.dma_start(out=brow[0:1, 0:128], in_=b1.rearrange("(o h) -> o h", o=1))
+                    nc.sync.dma_start(out=brow[0:1, 128:256], in_=b2.rearrange("(o h) -> o h", o=1))
+                    nc.sync.dma_start(out=brow[0:1, 256:384], in_=rr_uniform.rearrange("(o h) -> o h", o=1))
+                    load_w(0, W1)
+                if xi == 0 and c == 2:
                     load_w(1, W2)
             if xi == 0:
                 nc.sync.dma_start(out=nz[:], in_=noise_std.rearrange("(p t) h -> p (t h)", t=T_ALL))
@@ -75,16 +76,20 @@ def tile_splitnn_pa_t_kernel(tc, x1, x2, W1, b1, W2, b2, noise_std, rr_uniform, 
 
         ident = const.tile([P, P], F32)
         make_identity(nc, ident[:])
-
-        bc_ps = tpsum.tile([P, 512], F32, tag="tp", name="bc_ps")
-        nc.tensor.matmul(out=bc_ps[:], lhsT=ones[:], rhs=brow[:], start=True, stop=True)
-        b12 = const.tile([P, 256], F32)
+        b1f = const.tile([P, H], F32)
         keep = const.tile([P, H], F32)
-        nc.vector.tensor_copy(out=b12[:], in_=bc_ps[:, 0:256])
-        nc.vector.tensor_single_scalar(out=keep[:], in_=bc_ps[:, 256:384], scalar=P_KEEP, op=ALU.is_lt)
-        b1_b = b12[:, 0:128].unsqueeze(1).to_broadcast([P, T_CH, H])
-        b2_b = b12[:, 128:256].unsqueeze(1).to_broadcast([P, T_CH, H])
+        b2col = const.tile([P, 1], F32)
+        b1_b = b1f[:].unsqueeze(1).to_broadcast([P, T_CH, H])
         keep_b = keep[:].unsqueeze(1).to_broadcast([P, T_CH, H])
+
+        def spread_vectors():
+            bc_ps = apsum.tile([P, 512], F32, tag="acc", name="bc_ps")
+            nc.tensor.matmul(out=bc_ps[:], lhsT=ones[:, 0:P], rhs=brow[:], start=True, stop=True)
+            b2_ps = apsum.tile([P, 512], F32, tag="acc", name="b2_ps")
+            nc.tensor.matmul(out=b2_ps[:, 0:256], lhsT=brow[:, 128:256], rhs=ones[:], start=True, stop=True)
+            nc.vector.tensor_copy(out=b1f[:], in_=bc_ps[:, 0:128])
+            nc.vector.tensor_single_scalar(out=keep[:], in_=bc_ps[:, 256:384], scalar=P_KEEP, op=ALU.is_lt)
+            nc.vector.tensor_copy(out=b2col[:], in_=b2_ps[:, 0:1])
 
         wcs = []
 
@@ -102,8 +107,6 @@ def tile_splitnn_pa_t_kernel(tc, x1, x2, W1, b1, W2, b2, noise_std, rr_uniform, 
             wg, wc, ws = wcs[wi]
             nc.vector.quantize_mx(out=wc[:].bitcast(FP8X4), scales=ws[:], in_=wg[:])
 
-        prepare_w(0)
-
         a_all = const.tile([P, T_ALL * H], F32)
         nrm = const.tile([P, T_ALL], F32)
         mm = const.tile([P, 2], F32)
@@ -111,31 +114,36 @@ def tile_splitnn_pa_t_kernel(tc, x1, x2, W1, b1, W2, b2, noise_std, rr_uniform, 
         gm = const.tile([P, 2], F32)
         mul = const.tile([P, 1], F32)
 
-        quantise_w(0)
-
         banks = {}
         grps = {}
         codes = {}
+        accs = {}
         absd = {}
+        dts = {}
+        dns = {}
 
-        def transposes(i):
+        def transposes(i, which):
             xw = xs[i][:].bitcast(F32)
-            for t in range(T_CH):
-                bank = tpsum.tile([P, 512], F32, tag="tp", name="tp%d_%d" % (i, t))
+            for bk in which:
+                bank = tpsum.tile([P, 512], F32, tag="tp", name="tp%d_%d" % (i, bk))
                 for s in range(4):
-                    col = t * 512 + s * P
+                    if i < N_CH:
+                        col = bk * 512 + s * P
+                    else:
+                        col = (2 * (bk % 2) + s // 2) * 512 + (2 * (bk // 2) + s % 2) * P
                     nc.tensor.transpose(bank[:, s * P : (s + 1) * P], xw[:, col : col + P], ident[:])
-                banks[(i, t)] = bank
+                banks[(i, bk)] = bank
 
-        def evacuate(i):
-            grp = gpool.tile([P, T_CH * F], BF16, tag="grp", name="grp%d" % i, align_bytes=64)
-            gw = grp[:].bitcast(F32)
-            for t in range(T_CH):
-                nc.scalar.copy(
-                    out=gw[:, t * 512 : (t + 1) * 512].rearrange("p (g r u) -> p g r u", g=2, r=P, u=2),
-                    in_=banks[(i, t)][:].rearrange("p (g u r) -> p g r u", g=2, u=2, r=P),
-                )
-            grps[i] = grp
+        def evacuate(i, bk, on_vector):
+            if i not in grps:
+                grps[i] = gpool.tile([P, T_CH * F], BF16, tag="grp", name="grp%d" % i, align_bytes=64)
+            gw = grps[i][:].bitcast(F32)
+            dst = gw[:, bk * 512 : (bk + 1) * 512].rearrange("p (g r u) -> p g r u", g=2, r=P, u=2)
+            src = banks[(i, bk)][:].rearrange("p (g u r) -> p g r u", g=2, u=2, r=P)
+            if on_vector:
+                nc.vector.tensor_copy(out=dst, in_=src)
+            else:
+                nc.scalar.copy(out=dst, in_=src)
 
         def quantise(i):
             cd = qpool.tile([P, T_CH * 256], U32, tag="cd", name="cd%d" % i, align_bytes=64)
@@ -147,28 +155,44 @@ def tile_splitnn_pa_t_kernel(tc, x1, x2, W1, b1, W2, b2, noise_std, rr_uniform, 
             cd, sc = codes[i]
             wg, wc, ws = wcs[i // N_CH]
             acc = apsum.tile([P, 512], F32, tag="acc", name="acc%d" % i)
-            for t in range(T_CH):
+            if i < N_CH:
+                for t in range(T_CH):
+                    for g in range(2):
+                        col = (2 * t + g) * P
+                        nc.tensor.matmul_mx(
+                            out=acc[:, t * H : (t + 1) * H],
+                            lhsT=cd[:, col : col + P].bitcast(FP8X4),
+                            lhsT_scale=sc[:, col : col + P],
+                            rhs=wc[:, g * H : (g + 1) * H].bitcast(FP8X4),
+                            rhs_scale=ws[:, g * H : (g + 1) * H],
+                            start=(g == 0),
+                            stop=(g == 1),
+                        )
+            else:
                 for g in range(2):
-                    col = (2 * t + g) * P
                     nc.tensor.matmul_mx(
-                        out=acc[:, t * H : (t + 1) * H],
-                        lhsT=cd[:, col : col + P].bitcast(FP8X4),
-                        lhsT_scale=sc[:, col : col + P],
-                        rhs=wc[:, g * H : (g + 1) * H].bitcast(FP8X4),
-                        rhs_scale=ws[:, g * H : (g + 1) * H],
+                        out=acc[:],
+                        lhsT=wc[:, g * H : (g + 1) * H].bitcast(FP8X4),
+                        lhsT_scale=ws[:, g * H : (g + 1) * H],
+                        rhs=cd[:, g * 512 : (g + 1) * 512].bitcast(FP8X4),
+                        rhs_scale=sc[:, g * 512 : (g + 1) * 512],
                         start=(g == 0),
                         stop=(g == 1),
                     )
-            return acc
+            accs[i] = acc
 
         def three(ap):
             return ap.rearrange("p (t h) -> p t h", t=T_CH)
 
-        def finish_client1(c, acc):
-            a_c = a_all[:, c * 512 : (c + 1) * 512]
-            nc.vector.tensor_tensor(out=three(a_c), in0=three(acc[:]), in1=b1_b, op=ALU.add)
+        def a_chunk(c):
+            return a_all[:, c * 512 : (c + 1) * 512]
+
+        def add_b1(c):
+            nc.vector.tensor_tensor(out=three(a_chunk(c)), in0=three(accs[c][:]), in1=b1_b, op=ALU.add)
+
+        def absolute(c):
             ab = opool.tile([P, 512], F32, tag="ab", name="ab%d" % c)
-            nc.scalar.activation(out=ab[:], in_=a_c, func=ACT.Abs)
+            nc.scalar.activation(out=ab[:], in_=a_chunk(c), func=ACT.Abs)
             absd[c] = ab
 
         def norms(c):
@@ -176,8 +200,45 @@ def tile_splitnn_pa_t_kernel(tc, x1, x2, W1, b1, W2, b2, noise_std, rr_uniform, 
                 out=nrm[:, c * T_CH : (c + 1) * T_CH], in_=three(absd[c][:]), axis=AX.X, op=ALU.add
             )
 
-        def finish_client2(c, acc):
-            a_c = a_all[:, c * 512 : (c + 1) * 512]
+        def spread_a():
+            nc.vector.tensor_reduce(out=mm[:, 0:1], in_=nrm[:], axis=AX.X, op=ALU.max)
+            nc.vector.tensor_reduce(out=mm[:, 1:2], in_=nrm[:], axis=AX.X, op=ALU.min)
+            nc.vector.tensor_copy(
+                out=rep[:].rearrange("p (s j) -> p s j", s=2),
+                in_=mm[:].unsqueeze(2).to_broadcast([P, 2, P]),
+            )
+
+        def spread_b():
+            sp = tpsum.tile([P, 512], F32, tag="tp", name="sp")
+            nc.tensor.transpose(sp[:, 0:P], rep[:, 0:P], ident[:])
+            nc.tensor.transpose(sp[:, P : 2 * P], rep[:, P : 2 * P], ident[:])
+            return sp
+
+        def spread_c(sp):
+            nc.vector.tensor_reduce(out=gm[:, 0:1], in_=sp[:, 0:P], axis=AX.X, op=ALU.max)
+            nc.vector.tensor_reduce(out=gm[:, 1:2], in_=sp[:, P : 2 * P], axis=AX.X, op=ALU.min)
+            nc.vector.tensor_scalar(
+                out=mul[:],
+                in0=gm[:, 0:1],
+                scalar1=gm[:, 1:2],
+                scalar2=INV_EPS,
+                op0=ALU.subtract,
+                op1=ALU.mult,
+            )
+
+        def add_b2(c):
+            dt_ = opool.tile([P, 512], F32, tag="dt", name="dt%d" % c)
+            nc.scalar.activation(out=dt_[:], in_=accs[N_CH + c][:], func=ACT.Identity, bias=b2col[:, 0:1], scale=1.0)
+            dts[c] = dt_
+
+        def back(c):
+            dn = apsum.tile([P, 512], F32, tag="acc", name="dn%d" % c)
+            for t in range(T_CH):
+                nc.tensor.transpose(dn[:, t * P : (t + 1) * P], dts[c][:, t * P : (t + 1) * P], ident[:])
+            dns[c] = dn
+
+        def noisy(c):
+            a_c = a_chunk(c)
             nc.vector.scalar_tensor_tensor(
                 out=a_c,
                 in0=nz[:, c * 512 : (c + 1) * 512],
@@ -187,51 +248,63 @@ def tile_splitnn_pa_t_kernel(tc, x1, x2, W1, b1, W2, b2, noise_std, rr_uniform, 
                 op1=ALU.add,
             )
             nc.vector.tensor_tensor(out=three(a_c), in0=three(a_c), in1=keep_b, op=ALU.mult)
+
+        def minimum(c):
             o = opool.tile([P, 512], F32, tag="o", name="o%d" % c)
-            nc.vector.tensor_tensor(out=three(o[:]), in0=three(acc[:]), in1=b2_b, op=ALU.add)
-            nc.vector.tensor_tensor(out=o[:], in0=o[:], in1=a_c, op=ALU.min)
+            nc.vector.tensor_tensor(out=o[:], in0=dns[c][:], in1=a_chunk(c), op=ALU.min)
             nc.sync.dma_start(out=out_v[:, c * T_CH : (c + 1) * T_CH, :], in_=three(o[:]))
 
+        def on_vector(i, bk):
+            return i < N_CH and bk == 3 and i % 2 == 1
+
         n_all = 2 * N_CH
-        for i in range(n_all + 2):
+        sp = None
+        for i in range(n_all + 3):
+            first = 2 <= i < N_CH + 2
             if i < n_all:
-                transposes(i)
-                evacuate(i)
-            if i == N_CH + 2:
-                sp = tpsum.tile([P, 512], F32, tag="tp", name="sp")
-                nc.tensor.transpose(sp[:, 0:P], rep[:, 0:P], ident[:])
-                nc.tensor.transpose(sp[:, P : 2 * P], rep[:, P : 2 * P], ident[:])
+                if i == N_CH + 2:
+                    transposes(i, (0, 1))
+                    sp = spread_b()
+                    transposes(i, (2, 3))
+                else:
+                    transposes(i, (0, 1, 2, 3))
+            if i == 0:
+                spread_vectors()
+                prepare_w(0)
+            if i >= N_CH + 3:
+                back(i - N_CH - 3)
+            if 2 <= i < n_all + 2:
+                multiply(i - 2)
+            if i < n_all:
+                for bk in range(4):
+                    if on_vector(i, bk):
+                        evacuate(i, bk, True)
+            if first:
+                add_b1(i - 2)
+            if i < n_all:
+                mine = [bk for bk in range(4) if not on_vector(i, bk)]
+                for bk in mine[:2]:
+                    evacuate(i, bk, False)
+                if first:
+                    absolute(i - 2)
+                for bk in mine[2:]:
+                    evacuate(i, bk, False)
+            if N_CH + 2 <= i < n_all + 2:
+                add_b2(i - N_CH - 2)
+            if i == 0:
+                quantise_w(0)
             if i == 3:
                 prepare_w(1)
+            if i == N_CH + 2:
+                spread_c(sp)
             if 1 <= i <= n_all:
                 quantise(i - 1)
             if i == 3:
                 quantise_w(1)
-            if i == N_CH + 2:
-                nc.vector.tensor_reduce(out=gm[:, 0:1], in_=sp[:, 0:P], axis=AX.X, op=ALU.max)
-                nc.vector.tensor_reduce(out=gm[:, 1:2], in_=sp[:, P : 2 * P], axis=AX.X, op=ALU.min)
-                nc.vector.tensor_scalar(
-                    out=mul[:],
-                    in0=gm[:, 0:1],
-                    scalar1=gm[:, 1:2],
-                    scalar2=INV_EPS,
-                    op0=ALU.subtract,
-                    op1=ALU.mult,
-                )
-            if i >= 2:
-                j = i - 2
-                acc = multiply(j)
-                if j < N_CH:
-                    if j >= 1:
-                        norms(j - 1)
-                    finish_client1(j, acc)
-                else:
-                    finish_client2(j - N_CH, acc)
-                if j == N_CH - 1:
-                    norms(j)
-                    nc.vector.tensor_reduce(out=mm[:, 0:1], in_=nrm[:], axis=AX.X, op=ALU.max)
-                    nc.vector.tensor_reduce(out=mm[:, 1:2], in_=nrm[:], axis=AX.X, op=ALU.min)
-                    nc.vector.tensor_copy(
-                        out=rep[:].rearrange("p (s j) -> p s j", s=2),
-                        in_=mm[:].unsqueeze(2).to_broadcast([P, 2, P]),
-                    )
+            if first:
+                norms(i - 2)
+                if i - 2 == N_CH - 1:
+                    spread_a()
+            if i >= N_CH + 3:
+                noisy(i - N_CH - 3)
+                minimum(i - N_CH - 3)

@@ -31,8 +31,8 @@ def tile_splitnn_pa_t_kernel(tc, x1, x2, W1, b1, W2, b2, noise_std, rr_uniform, 
         gpool = ctx.enter_context(tc.tile_pool(name="gpool", bufs=3))
         qpool = ctx.enter_context(tc.tile_pool(name="qpool", bufs=3))
         opool = ctx.enter_context(tc.tile_pool(name="opool", bufs=3))
-        tpsum = ctx.enter_context(tc.psum_pool(name="tpsum", bufs=6))
-        apsum = ctx.enter_context(tc.psum_pool(name="apsum", bufs=2))
+        tpsum = ctx.enter_context(tc.psum_pool(name="tpsum", bufs=5))
+        apsum = ctx.enter_context(tc.psum_pool(name="apsum", bufs=3))
         ctx.enter_context(tc.manual_schedule())
 
         brow = const.tile([P, 512], BF16)
@@ -259,52 +259,50 @@ def tile_splitnn_pa_t_kernel(tc, x1, x2, W1, b1, W2, b2, noise_std, rr_uniform, 
 
         n_all = 2 * N_CH
         sp = None
-        for i in range(n_all + 3):
-            first = 2 <= i < N_CH + 2
+        for i in range(n_all + 4):
             if i < n_all:
-                if i == N_CH + 2:
-                    transposes(i, (0, 1))
-                    sp = spread_b()
-                    transposes(i, (2, 3))
-                else:
-                    transposes(i, (0, 1, 2, 3))
+                transposes(i, (0, 1, 2, 3))
             if i == 0:
                 spread_vectors()
                 prepare_w(0)
-            if i >= N_CH + 3:
-                back(i - N_CH - 3)
-            if 2 <= i < n_all + 2:
+            if 0 <= i - N_CH - 4 < N_CH:
+                back(i - N_CH - 4)
+            if i == N_CH + 3:
+                sp = spread_b()
+            if 0 <= i - 2 < n_all:
                 multiply(i - 2)
             if i < n_all:
                 for bk in range(4):
                     if on_vector(i, bk):
                         evacuate(i, bk, True)
-            if first:
-                add_b1(i - 2)
-            if i < n_all:
                 mine = [bk for bk in range(4) if not on_vector(i, bk)]
-                for bk in mine[:2]:
-                    evacuate(i, bk, False)
-                if first:
-                    absolute(i - 2)
-                for bk in mine[2:]:
-                    evacuate(i, bk, False)
-            if N_CH + 2 <= i < n_all + 2:
-                add_b2(i - N_CH - 2)
+            else:
+                mine = []
+            for bk in mine[:2]:
+                evacuate(i, bk, False)
+            if 0 <= i - 3 < N_CH:
+                absolute(i - 3)
+            if 0 <= i - N_CH - 3 < N_CH:
+                add_b2(i - N_CH - 3)
+            for bk in mine[2:]:
+                evacuate(i, bk, False)
             if i == 0:
                 quantise_w(0)
             if i == 3:
                 prepare_w(1)
-            if i == N_CH + 2:
+            if i == N_CH + 3:
                 spread_c(sp)
             if 1 <= i <= n_all:
                 quantise(i - 1)
             if i == 3:
                 quantise_w(1)
-            if first:
-                norms(i - 2)
-                if i - 2 == N_CH - 1:
-                    spread_a()
-            if i >= N_CH + 3:
+            if 0 <= i - N_CH - 4 < N_CH:
+                minimum(i - N_CH - 4)
+            if 0 <= i - N_CH - 3 < N_CH:
                 noisy(i - N_CH - 3)
-                minimum(i - N_CH - 3)
+            if 0 <= i - 2 < N_CH:
+                add_b1(i - 2)
+            if 0 <= i - 3 < N_CH:
+                norms(i - 3)
+                if i - 3 == N_CH - 1:
+                    spread_a()

@@ -32,7 +32,7 @@ def tile_splitnn_pa_t_kernel(tc, x1, x2, W1, b1, W2, b2, noise_std, rr_uniform, 
         qpool = ctx.enter_context(tc.tile_pool(name="qpool", bufs=3))
         opool = ctx.enter_context(tc.tile_pool(name="opool", bufs=3))
         tpsum = ctx.enter_context(tc.psum_pool(name="tpsum", bufs=5))
-        apsum = ctx.enter_context(tc.psum_pool(name="apsum", bufs=3))
+        apsum = ctx.enter_context(tc.psum_pool(name="apsum", bufs=2))
         ctx.enter_context(tc.manual_schedule())
 
         brow = const.tile([P, 512], BF16)
@@ -151,12 +151,14 @@ def tile_splitnn_pa_t_kernel(tc, x1, x2, W1, b1, W2, b2, noise_std, rr_uniform, 
             nc.vector.quantize_mx(out=cd[:].bitcast(FP8X4), scales=sc[:], in_=grps[i][:])
             codes[i] = (cd, sc)
 
-        def multiply(i):
+        def multiply(i, half):
             cd, sc = codes[i]
             wg, wc, ws = wcs[i // N_CH]
-            acc = apsum.tile([P, 512], F32, tag="acc", name="acc%d" % i)
+            if half == 0:
+                accs[i] = apsum.tile([P, 512], F32, tag="acc", name="acc%d" % i)
+            acc = accs[i]
             if i < N_CH:
-                for t in range(T_CH):
+                for t in (2 * half, 2 * half + 1):
                     for g in range(2):
                         col = (2 * t + g) * P
                         nc.tensor.matmul_mx(
@@ -169,7 +171,7 @@ def tile_splitnn_pa_t_kernel(tc, x1, x2, W1, b1, W2, b2, noise_std, rr_uniform, 
                             stop=(g == 1),
                         )
             else:
-                for g in range(2):
+                for g in (half,):
                     nc.tensor.matmul_mx(
                         out=acc[:],
                         lhsT=wc[:, g * H : (g + 1) * H].bitcast(FP8X4),
@@ -179,7 +181,6 @@ def tile_splitnn_pa_t_kernel(tc, x1, x2, W1, b1, W2, b2, noise_std, rr_uniform, 
                         start=(g == 0),
                         stop=(g == 1),
                     )
-            accs[i] = acc
 
         def three(ap):
             return ap.rearrange("p (t h) -> p t h", t=T_CH)
@@ -232,7 +233,7 @@ def tile_splitnn_pa_t_kernel(tc, x1, x2, W1, b1, W2, b2, noise_std, rr_uniform, 
             dts[c] = dt_
 
         def back(c):
-            dn = apsum.tile([P, 512], F32, tag="acc", name="dn%d" % c)
+            dn = apsum.tile([P, 512], F32, tag="dn", name="dn%d" % c, bufs=1)
             for t in range(T_CH):
                 nc.tensor.transpose(dn[:, t * P : (t + 1) * P], dts[c][:, t * P : (t + 1) * P], ident[:])
             dns[c] = dn
@@ -261,7 +262,11 @@ def tile_splitnn_pa_t_kernel(tc, x1, x2, W1, b1, W2, b2, noise_std, rr_uniform, 
         sp = None
         for i in range(n_all + 4):
             if i < n_all:
-                transposes(i, (0, 1, 2, 3))
+                transposes(i, (0, 1))
+            if 0 <= i - 2 < n_all:
+                multiply(i - 2, 0)
+            if i < n_all:
+                transposes(i, (2, 3))
             if i == 0:
                 spread_vectors()
                 prepare_w(0)
@@ -270,7 +275,7 @@ def tile_splitnn_pa_t_kernel(tc, x1, x2, W1, b1, W2, b2, noise_std, rr_uniform, 
             if i == N_CH + 3:
                 sp = spread_b()
             if 0 <= i - 2 < n_all:
-                multiply(i - 2)
+                multiply(i - 2, 1)
             if i < n_all:
                 for bk in range(4):
                     if on_vector(i, bk):

@@ -32,7 +32,7 @@ def tile_splitnn_pa_t_kernel(tc, x1, x2, W1, b1, W2, b2, noise_std, rr_uniform, 
         qpool = ctx.enter_context(tc.tile_pool(name="qpool", bufs=3))
         opool = ctx.enter_context(tc.tile_pool(name="opool", bufs=3))
         tpsum = ctx.enter_context(tc.psum_pool(name="tpsum", bufs=5))
-        apsum = ctx.enter_context(tc.psum_pool(name="apsum", bufs=2))
+        apsum = ctx.enter_context(tc.psum_pool(name="apsum", bufs=3))
         ctx.enter_context(tc.manual_schedule())
 
         brow = const.tile([P, 512], BF16)
@@ -70,14 +70,15 @@ def tile_splitnn_pa_t_kernel(tc, x1, x2, W1, b1, W2, b2, noise_std, rr_uniform, 
                     load_w(0, W1)
                 if xi == 0 and c == 2:
                     load_w(1, W2)
-            if xi == 0:
-                nc.sync.dma_start(out=nz[:], in_=noise_std.rearrange("(p t) h -> p (t h)", t=T_ALL))
+                if xi == 0 and c == 5:
+                    nc.sync.dma_start(out=nz[:], in_=noise_std.rearrange("(p t) h -> p (t h)", t=T_ALL))
         out_v = out.rearrange("(p t) h -> p t h", t=T_ALL)
 
         ident = const.tile([P, P], F32)
         make_identity(nc, ident[:])
         b1f = const.tile([P, H], F32)
         keep = const.tile([P, H], F32)
+        keep16 = const.tile([P, H], BF16)
         b2col = const.tile([P, 1], F32)
         b1_b = b1f[:].unsqueeze(1).to_broadcast([P, T_CH, H])
         keep_b = keep[:].unsqueeze(1).to_broadcast([P, T_CH, H])
@@ -89,6 +90,7 @@ def tile_splitnn_pa_t_kernel(tc, x1, x2, W1, b1, W2, b2, noise_std, rr_uniform, 
             nc.tensor.matmul(out=b2_ps[:, 0:256], lhsT=brow[:, 128:256], rhs=ones[:], start=True, stop=True)
             nc.vector.tensor_copy(out=b1f[:], in_=bc_ps[:, 0:128])
             nc.vector.tensor_single_scalar(out=keep[:], in_=bc_ps[:, 256:384], scalar=P_KEEP, op=ALU.is_lt)
+            nc.vector.tensor_single_scalar(out=keep16[:], in_=bc_ps[:, 256:384], scalar=P_KEEP, op=ALU.is_lt)
             nc.vector.tensor_copy(out=b2col[:], in_=b2_ps[:, 0:1])
 
         wcs = []
@@ -151,14 +153,12 @@ def tile_splitnn_pa_t_kernel(tc, x1, x2, W1, b1, W2, b2, noise_std, rr_uniform, 
             nc.vector.quantize_mx(out=cd[:].bitcast(FP8X4), scales=sc[:], in_=grps[i][:])
             codes[i] = (cd, sc)
 
-        def multiply(i, half):
+        def multiply(i):
             cd, sc = codes[i]
             wg, wc, ws = wcs[i // N_CH]
-            if half == 0:
-                accs[i] = apsum.tile([P, 512], F32, tag="acc", name="acc%d" % i)
-            acc = accs[i]
+            acc = apsum.tile([P, 512], F32, tag="acc", name="acc%d" % i)
             if i < N_CH:
-                for t in (2 * half, 2 * half + 1):
+                for t in range(T_CH):
                     for g in range(2):
                         col = (2 * t + g) * P
                         nc.tensor.matmul_mx(
@@ -171,7 +171,7 @@ def tile_splitnn_pa_t_kernel(tc, x1, x2, W1, b1, W2, b2, noise_std, rr_uniform, 
                             stop=(g == 1),
                         )
             else:
-                for g in (half,):
+                for g in range(2):
                     nc.tensor.matmul_mx(
                         out=acc[:],
                         lhsT=wc[:, g * H : (g + 1) * H].bitcast(FP8X4),
@@ -181,6 +181,7 @@ def tile_splitnn_pa_t_kernel(tc, x1, x2, W1, b1, W2, b2, noise_std, rr_uniform, 
                         start=(g == 0),
                         stop=(g == 1),
                     )
+            accs[i] = acc
 
         def three(ap):
             return ap.rearrange("p (t h) -> p t h", t=T_CH)
@@ -233,7 +234,7 @@ def tile_splitnn_pa_t_kernel(tc, x1, x2, W1, b1, W2, b2, noise_std, rr_uniform, 
             dts[c] = dt_
 
         def back(c):
-            dn = apsum.tile([P, 512], F32, tag="dn", name="dn%d" % c, bufs=1)
+            dn = apsum.tile([P, 512], F32, tag="acc", name="dn%d" % c)
             for t in range(T_CH):
                 nc.tensor.transpose(dn[:, t * P : (t + 1) * P], dts[c][:, t * P : (t + 1) * P], ident[:])
             dns[c] = dn
@@ -248,7 +249,16 @@ def tile_splitnn_pa_t_kernel(tc, x1, x2, W1, b1, W2, b2, noise_std, rr_uniform, 
                 op0=ALU.mult,
                 op1=ALU.add,
             )
-            nc.vector.tensor_tensor(out=three(a_c), in0=three(a_c), in1=keep_b, op=ALU.mult)
+
+        def mask_a(c):
+            a_c = a_chunk(c)
+            nc.gpsimd.tensor_tensor(out=three(a_c), in0=three(a_c), in1=keep_b, op=ALU.mult)
+
+        def mask_noise(q):
+            n_q = nz[:, q * 1024 : (q + 1) * 1024].rearrange("p (t h) -> p t h", t=2 * T_CH)
+            nc.vector.tensor_tensor(
+                out=n_q, in0=n_q, in1=keep16[:].unsqueeze(1).to_broadcast([P, 2 * T_CH, H]), op=ALU.mult
+            )
 
         def minimum(c):
             o = opool.tile([P, 512], F32, tag="o", name="o%d" % c)
@@ -262,11 +272,7 @@ def tile_splitnn_pa_t_kernel(tc, x1, x2, W1, b1, W2, b2, noise_std, rr_uniform, 
         sp = None
         for i in range(n_all + 4):
             if i < n_all:
-                transposes(i, (0, 1))
-            if 0 <= i - 2 < n_all:
-                multiply(i - 2, 0)
-            if i < n_all:
-                transposes(i, (2, 3))
+                transposes(i, (0, 1, 2, 3))
             if i == 0:
                 spread_vectors()
                 prepare_w(0)
@@ -275,7 +281,7 @@ def tile_splitnn_pa_t_kernel(tc, x1, x2, W1, b1, W2, b2, noise_std, rr_uniform, 
             if i == N_CH + 3:
                 sp = spread_b()
             if 0 <= i - 2 < n_all:
-                multiply(i - 2, 1)
+                multiply(i - 2)
             if i < n_all:
                 for bk in range(4):
                     if on_vector(i, bk):
@@ -291,6 +297,8 @@ def tile_splitnn_pa_t_kernel(tc, x1, x2, W1, b1, W2, b2, noise_std, rr_uniform, 
                 add_b2(i - N_CH - 3)
             for bk in mine[2:]:
                 evacuate(i, bk, False)
+            if 0 <= i - 3 < N_CH:
+                mask_a(i - 3)
             if i == 0:
                 quantise_w(0)
             if i == 3:
@@ -311,3 +319,5 @@ def tile_splitnn_pa_t_kernel(tc, x1, x2, W1, b1, W2, b2, noise_std, rr_uniform, 
                 norms(i - 3)
                 if i - 3 == N_CH - 1:
                     spread_a()
+            if 0 <= i - N_CH < 4:
+                mask_noise(i - N_CH)

@@ -52,7 +52,7 @@ def tile_splitnn_pa_t_kernel(tc, x1, x2, W1, b1, W2, b2, noise_std, rr_uniform, 
         xs = []
         nz = const.tile([P, T_ALL * H], BF16)
         for xi, x in enumerate((x1, x2)):
-            xv = x.rearrange("(p t) k -> p t k", t=T_ALL)
+            xv = x.rearrange("(c p t) k -> c p (t k)", c=N_CH, p=P, t=T_CH)
             for c in range(N_CH):
                 x_sb = xpool.tile([P, T_CH * F], BF16, tag="x", name="x%d_%d" % (xi, c))
                 pieces = 4 if (xi == 0 and c < 2) else 1
@@ -60,7 +60,7 @@ def tile_splitnn_pa_t_kernel(tc, x1, x2, W1, b1, W2, b2, noise_std, rr_uniform, 
                 for q in range(pieces):
                     nc.sync.dma_start(
                         out=x_sb[:, q * tp_ * F : (q + 1) * tp_ * F],
-                        in_=xv[:, c * T_CH + q * tp_ : c * T_CH + (q + 1) * tp_, :].rearrange("p t k -> p (t k)"),
+                        in_=xv[c][:, q * tp_ * F : (q + 1) * tp_ * F],
                     )
                 xs.append(x_sb)
                 if xi == 0 and c == 0:
@@ -71,8 +71,11 @@ def tile_splitnn_pa_t_kernel(tc, x1, x2, W1, b1, W2, b2, noise_std, rr_uniform, 
                 if xi == 0 and c == 2:
                     load_w(1, W2)
                 if xi == 0 and c == 5:
-                    nc.sync.dma_start(out=nz[:], in_=noise_std.rearrange("(p t) h -> p (t h)", t=T_ALL))
-        out_v = out.rearrange("(p t) h -> p t h", t=T_ALL)
+                    nc.sync.dma_start(
+                        out=nz[:].rearrange("p (c x) -> p c x", c=N_CH),
+                        in_=noise_std.rearrange("(c p t) h -> p c (t h)", c=N_CH, p=P, t=T_CH),
+                    )
+        out_v = out.rearrange("(c p t) h -> c p (t h)", c=N_CH, p=P, t=T_CH)
 
         ident = const.tile([P, P], F32)
         make_identity(nc, ident[:])
@@ -263,7 +266,7 @@ def tile_splitnn_pa_t_kernel(tc, x1, x2, W1, b1, W2, b2, noise_std, rr_uniform, 
         def minimum(c):
             o = opool.tile([P, 512], F32, tag="o", name="o%d" % c)
             nc.vector.tensor_tensor(out=o[:], in0=dns[c][:], in1=a_chunk(c), op=ALU.min)
-            nc.sync.dma_start(out=out_v[:, c * T_CH : (c + 1) * T_CH, :], in_=three(o[:]))
+            nc.sync.dma_start(out=out_v[c], in_=o[:])
 
         def on_vector(i, bk):
             return i < N_CH and bk == 3 and i % 2 == 1

@@ -52,7 +52,7 @@ def tile_splitnn_pa_t_kernel(tc, x1, x2, W1, b1, W2, b2, noise_std, rr_uniform, 
         xs = []
         nz = const.tile([P, T_ALL * H], BF16)
         for xi, x in enumerate((x1, x2)):
-            xv = x.rearrange("(c p t) k -> c p (t k)", c=N_CH, p=P, t=T_CH)
+            xv = x.rearrange("(p t) k -> p t k", t=T_ALL)
             for c in range(N_CH):
                 x_sb = xpool.tile([P, T_CH * F], BF16, tag="x", name="x%d_%d" % (xi, c))
                 pieces = 4 if (xi == 0 and c < 2) else 1
@@ -60,7 +60,7 @@ def tile_splitnn_pa_t_kernel(tc, x1, x2, W1, b1, W2, b2, noise_std, rr_uniform, 
                 for q in range(pieces):
                     nc.sync.dma_start(
                         out=x_sb[:, q * tp_ * F : (q + 1) * tp_ * F],
-                        in_=xv[c][:, q * tp_ * F : (q + 1) * tp_ * F],
+                        in_=xv[:, c * T_CH + q * tp_ : c * T_CH + (q + 1) * tp_, :].rearrange("p t k -> p (t k)"),
                     )
                 xs.append(x_sb)
                 if xi == 0 and c == 0:
@@ -70,12 +70,9 @@ def tile_splitnn_pa_t_kernel(tc, x1, x2, W1, b1, W2, b2, noise_std, rr_uniform, 
                     load_w(0, W1)
                 if xi == 0 and c == 2:
                     load_w(1, W2)
-                if xi == 0 and c == 5:
-                    nc.sync.dma_start(
-                        out=nz[:].rearrange("p (c x) -> p c x", c=N_CH),
-                        in_=noise_std.rearrange("(c p t) h -> p c (t h)", c=N_CH, p=P, t=T_CH),
-                    )
-        out_v = out.rearrange("(c p t) h -> c p (t h)", c=N_CH, p=P, t=T_CH)
+                if xi == 0 and c == N_CH - 1:
+                    nc.sync.dma_start(out=nz[:], in_=noise_std.rearrange("(p t) h -> p (t h)", t=T_ALL))
+        out_v = out.rearrange("(p t) h -> p t h", t=T_ALL)
 
         ident = const.tile([P, P], F32)
         make_identity(nc, ident[:])
@@ -114,6 +111,7 @@ def tile_splitnn_pa_t_kernel(tc, x1, x2, W1, b1, W2, b2, noise_std, rr_uniform, 
 
         a_all = const.tile([P, T_ALL * H], F32)
         nrm = const.tile([P, T_ALL], F32)
+        junk = const.tile([P, H], F32)
         mm = const.tile([P, 2], F32)
         rep = const.tile([P, 256], F32)
         gm = const.tile([P, 2], F32)
@@ -196,14 +194,11 @@ def tile_splitnn_pa_t_kernel(tc, x1, x2, W1, b1, W2, b2, noise_std, rr_uniform, 
             nc.vector.tensor_tensor(out=three(a_chunk(c)), in0=three(accs[c][:]), in1=b1_b, op=ALU.add)
 
         def absolute(c):
-            ab = opool.tile([P, 512], F32, tag="ab", name="ab%d" % c)
-            nc.scalar.activation(out=ab[:], in_=a_chunk(c), func=ACT.Abs)
-            absd[c] = ab
-
-        def norms(c):
-            nc.vector.tensor_reduce(
-                out=nrm[:, c * T_CH : (c + 1) * T_CH], in_=three(absd[c][:]), axis=AX.X, op=ALU.add
-            )
+            for t in range(T_CH):
+                col = c * T_CH + t
+                nc.scalar.activation(
+                    out=junk[:], in_=a_all[:, col * H : (col + 1) * H], func=ACT.Abs, accum_out=nrm[:, col : col + 1]
+                )
 
         def spread_a():
             nc.vector.tensor_reduce(out=mm[:, 0:1], in_=nrm[:], axis=AX.X, op=ALU.max)
@@ -266,10 +261,10 @@ def tile_splitnn_pa_t_kernel(tc, x1, x2, W1, b1, W2, b2, noise_std, rr_uniform, 
         def minimum(c):
             o = opool.tile([P, 512], F32, tag="o", name="o%d" % c)
             nc.vector.tensor_tensor(out=o[:], in0=dns[c][:], in1=a_chunk(c), op=ALU.min)
-            nc.sync.dma_start(out=out_v[c], in_=o[:])
+            nc.sync.dma_start(out=out_v[:, c * T_CH : (c + 1) * T_CH, :], in_=three(o[:]))
 
         def on_vector(i, bk):
-            return i < N_CH and bk == 3 and i % 2 == 1
+            return i < N_CH + 2 and bk == 3
 
         n_all = 2 * N_CH
         sp = None
@@ -285,13 +280,7 @@ def tile_splitnn_pa_t_kernel(tc, x1, x2, W1, b1, W2, b2, noise_std, rr_uniform, 
                 sp = spread_b()
             if 0 <= i - 2 < n_all:
                 multiply(i - 2)
-            if i < n_all:
-                for bk in range(4):
-                    if on_vector(i, bk):
-                        evacuate(i, bk, True)
-                mine = [bk for bk in range(4) if not on_vector(i, bk)]
-            else:
-                mine = []
+            mine = [bk for bk in range(4) if not on_vector(i, bk)] if i < n_all else []
             for bk in mine[:2]:
                 evacuate(i, bk, False)
             if 0 <= i - 3 < N_CH:
@@ -312,15 +301,17 @@ def tile_splitnn_pa_t_kernel(tc, x1, x2, W1, b1, W2, b2, noise_std, rr_uniform, 
                 quantise(i - 1)
             if i == 3:
                 quantise_w(1)
+            if i < n_all:
+                for bk in range(4):
+                    if on_vector(i, bk):
+                        evacuate(i, bk, True)
             if 0 <= i - N_CH - 4 < N_CH:
                 minimum(i - N_CH - 4)
             if 0 <= i - N_CH - 3 < N_CH:
                 noisy(i - N_CH - 3)
             if 0 <= i - 2 < N_CH:
                 add_b1(i - 2)
-            if 0 <= i - 3 < N_CH:
-                norms(i - 3)
-                if i - 3 == N_CH - 1:
-                    spread_a()
-            if 0 <= i - N_CH < 4:
-                mask_noise(i - N_CH)
+            if i - 3 == N_CH - 1:
+                spread_a()
+            if 0 <= i - N_CH - 1 < 4:
+                mask_noise(i - N_CH - 1)

@@ -33,7 +33,6 @@ def tile_splitnn_pa_t_kernel(tc, x1, x2, W1, b1, W2, b2, noise_std, rr_uniform, 
         opool = ctx.enter_context(tc.tile_pool(name="opool", bufs=3))
         tpsum = ctx.enter_context(tc.psum_pool(name="tpsum", bufs=5))
         apsum = ctx.enter_context(tc.psum_pool(name="apsum", bufs=3))
-        ctx.enter_context(tc.manual_schedule())
 
         brow = const.tile([P, 512], BF16)
         ones = const.tile([P, 256], BF16)
@@ -70,7 +69,7 @@ def tile_splitnn_pa_t_kernel(tc, x1, x2, W1, b1, W2, b2, noise_std, rr_uniform, 
                     load_w(0, W1)
                 if xi == 0 and c == 2:
                     load_w(1, W2)
-                if xi == 0 and c == N_CH - 1:
+                if xi == 0 and c == 5:
                     nc.sync.dma_start(out=nz[:], in_=noise_std.rearrange("(p t) h -> p (t h)", t=T_ALL))
         out_v = out.rearrange("(p t) h -> p t h", t=T_ALL)
 
@@ -111,7 +110,6 @@ def tile_splitnn_pa_t_kernel(tc, x1, x2, W1, b1, W2, b2, noise_std, rr_uniform, 
 
         a_all = const.tile([P, T_ALL * H], F32)
         nrm = const.tile([P, T_ALL], F32)
-        junk = const.tile([P, H], F32)
         mm = const.tile([P, 2], F32)
         rep = const.tile([P, 256], F32)
         gm = const.tile([P, 2], F32)
@@ -194,11 +192,14 @@ def tile_splitnn_pa_t_kernel(tc, x1, x2, W1, b1, W2, b2, noise_std, rr_uniform, 
             nc.vector.tensor_tensor(out=three(a_chunk(c)), in0=three(accs[c][:]), in1=b1_b, op=ALU.add)
 
         def absolute(c):
-            for t in range(T_CH):
-                col = c * T_CH + t
-                nc.scalar.activation(
-                    out=junk[:], in_=a_all[:, col * H : (col + 1) * H], func=ACT.Abs, accum_out=nrm[:, col : col + 1]
-                )
+            ab = opool.tile([P, 512], F32, tag="ab", name="ab%d" % c)
+            nc.scalar.activation(out=ab[:], in_=a_chunk(c), func=ACT.Abs)
+            absd[c] = ab
+
+        def norms(c):
+            nc.vector.tensor_reduce(
+                out=nrm[:, c * T_CH : (c + 1) * T_CH], in_=three(absd[c][:]), axis=AX.X, op=ALU.add
+            )
 
         def spread_a():
             nc.vector.tensor_reduce(out=mm[:, 0:1], in_=nrm[:], axis=AX.X, op=ALU.max)
@@ -264,7 +265,7 @@ def tile_splitnn_pa_t_kernel(tc, x1, x2, W1, b1, W2, b2, noise_std, rr_uniform, 
             nc.sync.dma_start(out=out_v[:, c * T_CH : (c + 1) * T_CH, :], in_=three(o[:]))
 
         def on_vector(i, bk):
-            return i < N_CH + 2 and bk == 3
+            return i < N_CH and bk == 3 and i % 2 == 1
 
         n_all = 2 * N_CH
         sp = None
@@ -280,7 +281,13 @@ def tile_splitnn_pa_t_kernel(tc, x1, x2, W1, b1, W2, b2, noise_std, rr_uniform, 
                 sp = spread_b()
             if 0 <= i - 2 < n_all:
                 multiply(i - 2)
-            mine = [bk for bk in range(4) if not on_vector(i, bk)] if i < n_all else []
+            if i < n_all:
+                for bk in range(4):
+                    if on_vector(i, bk):
+                        evacuate(i, bk, True)
+                mine = [bk for bk in range(4) if not on_vector(i, bk)]
+            else:
+                mine = []
             for bk in mine[:2]:
                 evacuate(i, bk, False)
             if 0 <= i - 3 < N_CH:
@@ -301,17 +308,15 @@ def tile_splitnn_pa_t_kernel(tc, x1, x2, W1, b1, W2, b2, noise_std, rr_uniform, 
                 quantise(i - 1)
             if i == 3:
                 quantise_w(1)
-            if i < n_all:
-                for bk in range(4):
-                    if on_vector(i, bk):
-                        evacuate(i, bk, True)
             if 0 <= i - N_CH - 4 < N_CH:
                 minimum(i - N_CH - 4)
             if 0 <= i - N_CH - 3 < N_CH:
                 noisy(i - N_CH - 3)
             if 0 <= i - 2 < N_CH:
                 add_b1(i - 2)
-            if i - 3 == N_CH - 1:
-                spread_a()
-            if 0 <= i - N_CH - 1 < 4:
-                mask_noise(i - N_CH - 1)
+            if 0 <= i - 3 < N_CH:
+                norms(i - 3)
+                if i - 3 == N_CH - 1:
+                    spread_a()
+            if 0 <= i - N_CH < 4:
+                mask_noise(i - N_CH)

from contextlib import ExitStack

import concourse.mybir as mybir
from concourse.masks import make_identity

F32 = mybir.dt.float32
BF16 = mybir.dt.bfloat16
U32 = mybir.dt.uint32
U8 = mybir.dt.uint8
FP8X4 = mybir.dt.float8_e4m3fn_x4
ALU = mybir.AluOpType
AX = mybir.AxisListType
ACT = mybir.ActivationFunctionType

P = 128
B, F, H = 4096, 1024, 128
T_ALL = B // P
T_CH = 4
N_CH = T_ALL // T_CH
INV_EPS = 7.5
P_KEEP = 0.95

FLOPS = 2 * 2 * B * F * H


def tile_splitnn_pa_t_kernel(tc, x1, x2, W1, b1, W2, b2, noise_std, rr_uniform, out):
    nc = tc.nc
    with ExitStack() as ctx:
        const = ctx.enter_context(tc.tile_pool(name="const", bufs=1))
        xpool = ctx.enter_context(tc.tile_pool(name="xpool", bufs=2 * N_CH))
        gpool = ctx.enter_context(tc.tile_pool(name="gpool", bufs=3))
        qpool = ctx.enter_context(tc.tile_pool(name="qpool", bufs=3))
        opool = ctx.enter_context(tc.tile_pool(name="opool", bufs=3))
        tpsum = ctx.enter_context(tc.psum_pool(name="tpsum", bufs=5))
        apsum = ctx.enter_context(tc.psum_pool(name="apsum", bufs=3))

        brow = const.tile([P, 512], BF16)
        ones = const.tile([P, 256], BF16)
        nc.vector.memset(brow[:], 0.0)
        nc.vector.memset(ones[:], 1.0)
        wraws = []

        def load_w(wi, W):
            wraw = const.tile([P, 1024], BF16, name="wraw%d" % wi)
            nc.sync.dma_start(
                out=wraw[:].rearrange("p (s e h) -> p s e h", s=4, e=2),
                in_=W.rearrange("(s q e) h -> q s e h", s=4, q=P, e=2),
            )
            wraws.append(wraw)

        xs = []
        nz = const.tile([P, T_ALL * H], BF16)
        for xi, x in enumerate((x1, x2)):
            xv = x.rearrange("(p t) k -> p t k", t=T_ALL)
            for c in range(N_CH):
                x_sb = xpool.tile([P, T_CH * F], BF16, tag="x", name="x%d_%d" % (xi, c))
                pieces = 4 if (xi == 0 and c < 2) else 1
                tp_ = T_CH // pieces
                for q in range(pieces):
                    nc.sync.dma_start(
                        out=x_sb[:, q * tp_ * F : (q + 1) * tp_ * F],
                        in_=xv[:, c * T_CH + q * tp_ : c * T_CH + (q + 1) * tp_, :].rearrange("p t k -> p (t k)"),
                    )
                xs.append(x_sb)
                if xi == 0 and c == 0:
                    nc.sync.dma_start(out=brow[0:1, 0:128], in_=b1.rearrange("(o h) -> o h", o=1))
                    nc.sync.dma_start(out=brow[0:1, 128:256], in_=b2.rearrange("(o h) -> o h", o=1))
                    nc.sync.dma_start(out=brow[0:1, 256:384], in_=rr_uniform.rearrange("(o h) -> o h", o=1))
                    load_w(0, W1)
                if xi == 0 and c == 2:
                    load_w(1, W2)
                if xi == 0 and c == 5:
                    nc.sync.dma_start(out=nz[:], in_=noise_std.rearrange("(p t) h -> p (t h)", t=T_ALL))
        out_v = out.rearrange("(p t) h -> p t h", t=T_ALL)

        ident = const.tile([P, P], F32)
        make_identity(nc, ident[:])
        b1f = const.tile([P, H], F32)
        keep = const.tile([P, H], F32)
        keep16 = const.tile([P, H], BF16)
        b2col = const.tile([P, 1], F32)
        b1_b = b1f[:].unsqueeze(1).to_broadcast([P, T_CH, H])
        keep_b = keep[:].unsqueeze(1).to_broadcast([P, T_CH, H])

        def spread_vectors():
            bc_ps = apsum.tile([P, 512], F32, tag="acc", name="bc_ps")
            nc.tensor.matmul(out=bc_ps[:], lhsT=ones[:, 0:P], rhs=brow[:], start=True, stop=True)
            b2_ps = apsum.tile([P, 512], F32, tag="acc", name="b2_ps")
            nc.tensor.matmul(out=b2_ps[:, 0:256], lhsT=brow[:, 128:256], rhs=ones[:], start=True, stop=True)
            nc.vector.tensor_copy(out=b1f[:], in_=bc_ps[:, 0:128])
            nc.vector.tensor_single_scalar(out=keep[:], in_=bc_ps[:, 256:384], scalar=P_KEEP, op=ALU.is_lt)
            nc.vector.tensor_single_scalar(out=keep16[:], in_=bc_ps[:, 256:384], scalar=P_KEEP, op=ALU.is_lt)
            nc.vector.tensor_copy(out=b2col[:], in_=b2_ps[:, 0:1])

        wcs = []

        def prepare_w(wi):
            wg = const.tile([P, 1024], BF16, name="wg%d" % wi, align_bytes=64)
            nc.vector.tensor_copy(
                out=wg[:].rearrange("p (g h t) -> p g h t", g=2, h=H, t=4),
                in_=wraws[wi][:].rearrange("p (g t h) -> p g h t", g=2, t=4, h=H),
            )
            wc = const.tile([P, 256], U32, name="wc%d" % wi, align_bytes=64)
            ws = const.tile([P, 256], U8, name="ws%d" % wi, align_bytes=64)
            wcs.append((wg, wc, ws))

        def quantise_w(wi):
            wg, wc, ws = wcs[wi]
            nc.vector.quantize_mx(out=wc[:].bitcast(FP8X4), scales=ws[:], in_=wg[:])

        a_all = const.tile([P, T_ALL * H], F32)
        nrm = const.tile([P, T_ALL], F32)
        mm = const.tile([P, 2], F32)
        rep = const.tile([P, 256], F32)
        gm = const.tile([P, 2], F32)
        mul = const.tile([P, 1], F32)

        banks = {}
        grps = {}
        codes = {}
        accs = {}
        absd = {}
        dts = {}
        dns = {}

        def transposes(i, which):
            xw = xs[i][:].bitcast(F32)
            for bk in which:
                bank = tpsum.tile([P, 512], F32, tag="tp", name="tp%d_%d" % (i, bk))
                for s in range(4):
                    if i < N_CH:
                        col = bk * 512 + s * P
                    else:
                        col = (2 * (bk % 2) + s // 2) * 512 + (2 * (bk // 2) + s % 2) * P
                    nc.tensor.transpose(bank[:, s * P : (s + 1) * P], xw[:, col : col + P], ident[:])
                banks[(i, bk)] = bank

        def evacuate(i, bk, on_vector):
            if i not in grps:
                grps[i] = gpool.tile([P, T_CH * F], BF16, tag="grp", name="grp%d" % i, align_bytes=64)
            gw = grps[i][:].bitcast(F32)
            dst = gw[:, bk * 512 : (bk + 1) * 512].rearrange("p (g r u) -> p g r u", g=2, r=P, u=2)
            src = banks[(i, bk)][:].rearrange("p (g u r) -> p g r u", g=2, u=2, r=P)
            if on_vector:
                nc.vector.tensor_copy(out=dst, in_=src)
            else:
                nc.scalar.copy(out=dst, in_=src)

        def quantise(i):
            cd = qpool.tile([P, T_CH * 256], U32, tag="cd", name="cd%d" % i, align_bytes=64)
            sc = qpool.tile([P, T_CH * 256], U8, tag="sc", name="sc%d" % i, align_bytes=64)
            nc.vector.quantize_mx(out=cd[:].bitcast(FP8X4), scales=sc[:], in_=grps[i][:])
            codes[i] = (cd, sc)

        def multiply(i):
            cd, sc = codes[i]
            wg, wc, ws = wcs[i // N_CH]
            acc = apsum.tile([P, 512], F32, tag="acc", name="acc%d" % i)
            if i < N_CH:
                for t in range(T_CH):
                    for g in range(2):
                        col = (2 * t + g) * P
                        nc.tensor.matmul_mx(
                            out=acc[:, t * H : (t + 1) * H],
                            lhsT=cd[:, col : col + P].bitcast(FP8X4),
                            lhsT_scale=sc[:, col : col + P],
                            rhs=wc[:, g * H : (g + 1) * H].bitcast(FP8X4),
                            rhs_scale=ws[:, g * H : (g + 1) * H],
                            start=(g == 0),
                            stop=(g == 1),
                        )
            else:
                for g in range(2):
                    nc.tensor.matmul_mx(
                        out=acc[:],
                        lhsT=wc[:, g * H : (g + 1) * H].bitcast(FP8X4),
                        lhsT_scale=ws[:, g * H : (g + 1) * H],
                        rhs=cd[:, g * 512 : (g + 1) * 512].bitcast(FP8X4),
                        rhs_scale=sc[:, g * 512 : (g + 1) * 512],
                        start=(g == 0),
                        stop=(g == 1),
                    )
            accs[i] = acc

        def three(ap):
            return ap.rearrange("p (t h) -> p t h", t=T_CH)

        def a_chunk(c):
            return a_all[:, c * 512 : (c + 1) * 512]

        def add_b1(c):
            nc.vector.tensor_tensor(out=three(a_chunk(c)), in0=three(accs[c][:]), in1=b1_b, op=ALU.add)

        def absolute(c):
            ab = opool.tile([P, 512], F32, tag="ab", name="ab%d" % c)
            nc.scalar.activation(out=ab[:], in_=a_chunk(c), func=ACT.Abs)
            absd[c] = ab

        def norms(c):
            nc.vector.tensor_reduce(
                out=nrm[:, c * T_CH : (c + 1) * T_CH], in_=three(absd[c][:]), axis=AX.X, op=ALU.add
            )

        def spread_a():
            nc.vector.tensor_reduce(out=mm[:, 0:1], in_=nrm[:], axis=AX.X, op=ALU.max)
            nc.vector.tensor_reduce(out=mm[:, 1:2], in_=nrm[:], axis=AX.X, op=ALU.min)
            nc.vector.tensor_copy(
                out=rep[:].rearrange("p (s j) -> p s j", s=2),
                in_=mm[:].unsqueeze(2).to_broadcast([P, 2, P]),
            )

        def spread_b():
            sp = tpsum.tile([P, 512], F32, tag="tp", name="sp")
            nc.tensor.transpose(sp[:, 0:P], rep[:, 0:P], ident[:])
            nc.tensor.transpose(sp[:, P : 2 * P], rep[:, P : 2 * P], ident[:])
            return sp

        def spread_c(sp):
            nc.vector.tensor_reduce(out=gm[:, 0:1], in_=sp[:, 0:P], axis=AX.X, op=ALU.max)
            nc.vector.tensor_reduce(out=gm[:, 1:2], in_=sp[:, P : 2 * P], axis=AX.X, op=ALU.min)
            nc.vector.tensor_scalar(
                out=mul[:],
                in0=gm[:, 0:1],
                scalar1=gm[:, 1:2],
                scalar2=INV_EPS,
                op0=ALU.subtract,
                op1=ALU.mult,
            )

        def add_b2(c):
            dt_ = opool.tile([P, 512], F32, tag="dt", name="dt%d" % c)
            nc.scalar.activation(out=dt_[:], in_=accs[N_CH + c][:], func=ACT.Identity, bias=b2col[:, 0:1], scale=1.0)
            dts[c] = dt_

        def back(c):
            dn = apsum.tile([P, 512], F32, tag="acc", name="dn%d" % c)
            for t in range(T_CH):
                nc.tensor.transpose(dn[:, t * P : (t + 1) * P], dts[c][:, t * P : (t + 1) * P], ident[:])
            dns[c] = dn

        def noisy(c):
            a_c = a_chunk(c)
            nc.vector.scalar_tensor_tensor(
                out=a_c,
                in0=nz[:, c * 512 : (c + 1) * 512],
                scalar=mul[:, 0:1],
                in1=a_c,
                op0=ALU.mult,
                op1=ALU.add,
            )

        def mask_a(c):
            a_c = a_chunk(c)
            nc.gpsimd.tensor_tensor(out=three(a_c), in0=three(a_c), in1=keep_b, op=ALU.mult)

        def mask_noise(q):
            n_q = nz[:, q * 1024 : (q + 1) * 1024].rearrange("p (t h) -> p t h", t=2 * T_CH)
            nc.vector.tensor_tensor(
                out=n_q, in0=n_q, in1=keep16[:].unsqueeze(1).to_broadcast([P, 2 * T_CH, H]), op=ALU.mult
            )

        def minimum(c):
            o = opool.tile([P, 512], F32, tag="o", name="o%d" % c)
            nc.vector.tensor_tensor(out=o[:], in0=dns[c][:], in1=a_chunk(c), op=ALU.min)
            nc.sync.dma_start(out=out_v[:, c * T_CH : (c + 1) * T_CH, :], in_=three(o[:]))

        def on_vector(i, bk):
            return i < N_CH and bk == 3 and i % 2 == 1

        n_all = 2 * N_CH
        sp = None
        for i in range(n_all + 4):
            if i < n_all:
                transposes(i, (0, 1, 2, 3))
            if i == 0:
                spread_vectors()
                prepare_w(0)
            if 0 <= i - N_CH - 4 < N_CH:
                back(i - N_CH - 4)
            if i == N_CH + 3:
                sp = spread_b()
            if 0 <= i - 2 < n_all:
                multiply(i - 2)
            if i < n_all:
                for bk in range(4):
                    if on_vector(i, bk):
                        evacuate(i, bk, True)
                mine = [bk for bk in range(4) if not on_vector(i, bk)]
            else:
                mine = []
            for bk in mine[:2]:
                evacuate(i, bk, False)
            if 0 <= i - 3 < N_CH:
                absolute(i - 3)
            if 0 <= i - N_CH - 3 < N_CH:
                add_b2(i - N_CH - 3)
            for bk in mine[2:]:
                evacuate(i, bk, False)
            if 0 <= i - 3 < N_CH:
                mask_a(i - 3)
            if i == 0:
                quantise_w(0)
            if i == 3:
                prepare_w(1)
            if i == N_CH + 3:
                spread_c(sp)
            if 1 <= i <= n_all:
                quantise(i - 1)
            if i == 3:
                quantise_w(1)
            if 0 <= i - N_CH - 4 < N_CH:
                minimum(i - N_CH - 4)
            if 0 <= i - N_CH - 3 < N_CH:
                noisy(i - N_CH - 3)
            if 0 <= i - 2 < N_CH:
                add_b1(i - 2)
            if 0 <= i - 3 < N_CH:
                norms(i - 3)
                if i - 3 == N_CH - 1:
                    spread_a()
            if 0 <= i - N_CH < 4:
                mask_noise(i - N_CH)
